import numpy as np
import ml_dtypes


def mxq(x, axis, fmt="e4m3"):
    dtype, down = {"e4m3": (ml_dtypes.float8_e4m3fn, 7), "e5m2": (ml_dtypes.float8_e5m2, 14)}[fmt]
    v = np.moveaxis(np.asarray(x, np.float32).astype(ml_dtypes.bfloat16).astype(np.float64), axis, -1)
    blocks = v.reshape(v.shape[:-1] + (-1, 32))
    amax = np.abs(blocks).max(-1, keepdims=True)
    byte = np.maximum(np.where(amax > 0, np.frexp(amax)[1] - 1 + 127, 0) - down, 1)
    scale = np.exp2(byte - 127.0)
    codes = (blocks / scale).astype(np.float32).astype(dtype).astype(np.float64)
    return np.moveaxis((codes * scale).reshape(v.shape), -1, axis)


WIDE = False


def mx_kscale(k):
    if not WIDE:
        return np.ones(k)
    levels = np.array([10, -10, 5, -5, 0])
    if k % 512:
        return np.exp2(np.random.permutation(np.resize(levels, k // 32))).repeat(32)
    a = np.empty((k // 512, 16))
    for p in range(k // 512):
        a[p, :8] = np.random.permutation(np.resize(levels, 8))
        for g in range(8):
            far = levels[np.abs(levels - a[p, g]) >= 10]
            a[p, g + 8] = far[np.random.randint(len(far))]
    return np.exp2(a.ravel()).repeat(32)


BF16 = ml_dtypes.bfloat16


def bf(x):
    return np.asarray(x, np.float32).astype(BF16)


def f64(x):
    return np.asarray(x).astype(np.float64)


B, D, H = 8192, 512, 8
DH = D // H
LN_EPS = 1e-5


def layernorm(x, g, b):
    mu = x.mean(-1, keepdims=True)
    var = ((x - mu) ** 2).mean(-1, keepdims=True)
    return (x - mu) / np.sqrt(var + LN_EPS) * g + b


def draw0():
    s, t = mx_kscale(D), mx_kscale(D)
    return {"kv_in": bf(np.random.standard_normal((B, D)) * s),
            "q_in": bf(np.random.standard_normal((B, D))),
            "attn_w": bf(np.random.uniform(0.25, 1.0, (B, H, 1))),
            "w_v": bf(np.random.standard_normal((D, D)) / np.sqrt(D) / s[None, :] * t[:, None]),
            "b_v": bf(np.random.standard_normal(D) * 0.3 * t),
            "out_w": bf(np.random.standard_normal((D, D)) / np.sqrt(D) / t[None, :]),
            "out_b": bf(np.random.standard_normal(D) * 0.3),
            "ln_g": bf(1.0 + 0.1 * np.random.standard_normal(D)),
            "ln_b": bf(0.1 * np.random.standard_normal(D))}


def core(kv_in, q_in, attn_w, w_v, b_v, out_w, out_b, ln_g, ln_b):
    v = ((mxq(f64(kv_in), 1, "e4m3") @ mxq(f64(w_v), 1, "e4m3").T) + f64(b_v)).reshape(B, H, DH)
    attn = (f64(attn_w) * v).reshape(B, D)
    y = (mxq(attn, 1, "e4m3") @ mxq(f64(out_w), 1, "e4m3").T) + f64(out_b)
    return layernorm(y + f64(q_in), f64(ln_g), f64(ln_b))


def e4m3fn_bytes(y):
    return np.clip(np.asarray(y, np.float64), -448.0, 448.0).astype(np.float32).astype(ml_dtypes.float8_e4m3fn).view(np.uint8)


def e4m3fn_values(b):
    return np.asarray(b, np.uint8).view(ml_dtypes.float8_e4m3fn).astype(np.float64)


def setup_inputs():
    d = draw0()
    x0 = np.asarray(d['kv_in']).astype(np.float64)
    s = (np.max(np.abs(x0), axis=(0,), keepdims=True) / 448.0).astype(np.float32)
    out = {}
    for k, v in d.items():
        if k == 'kv_in':
            out['kv_in_bytes'] = e4m3fn_bytes(x0 / s.astype(np.float64))
            out['kv_in_scale'] = s
        else:
            out[k] = v
    return out


def reference(kv_in_bytes, kv_in_scale, q_in, attn_w, w_v, b_v, out_w, out_b, ln_g, ln_b):
    return core(e4m3fn_values(kv_in_bytes) * kv_in_scale.astype(np.float64), q_in, attn_w, w_v, b_v, out_w, out_b, ln_g, ln_b)

@@ -1,0 +1,362 @@
+from contextlib import ExitStack
+
+import concourse.mybir as mybir
+from concourse.masks import make_identity
+
+ROWS, D, HEADS = 8192, 512, 8
+FLOPS = 2 * 2 * ROWS * D * D
+LN_EPS = 1e-5
+
+F32 = mybir.dt.float32
+BF16 = mybir.dt.bfloat16
+U32 = mybir.dt.uint32
+U8 = mybir.dt.uint8
+FP8 = mybir.dt.float8_e4m3fn
+FP8X4 = mybir.dt.float8_e4m3fn_x4
+ACT = mybir.ActivationFunctionType
+ALU = mybir.AluOpType
+
+P = 128
+T = 4
+LANES = P // HEADS
+SIZES = (2,) + (4,) * 15 + (2,)
+GROUPS = len(SIZES)
+STARTS = tuple(sum(SIZES[:g]) for g in range(GROUPS))
+
+
+def tile_crossmodalattention_pa_t_kernel(
+    tc, kv_in_bytes, kv_in_scale, q_in, attn_w, w_v, b_v, out_w, out_b, ln_g, ln_b, out
+):
+    nc = tc.nc
+
+    def rows_of(tensor, g):
+        return tensor[STARTS[g] * P : (STARTS[g] + SIZES[g]) * P, :].rearrange("(p j) n -> p j n", j=SIZES[g])
+
+    with ExitStack() as ctx:
+        const = ctx.enter_context(tc.tile_pool(name="const", bufs=1))
+        two = ctx.enter_context(tc.tile_pool(name="two", bufs=2))
+        three = ctx.enter_context(tc.tile_pool(name="three", bufs=3))
+        four = ctx.enter_context(tc.tile_pool(name="four", bufs=4))
+        ps_s = ctx.enter_context(tc.psum_pool(name="ps_s", bufs=4))
+        ps_v = ctx.enter_context(tc.psum_pool(name="ps_v", bufs=4))
+        ctx.enter_context(tc.manual_schedule())
+
+        kb = {}
+        q = {}
+        kvb = {}
+        xt = {}
+        grp = {}
+        aw = {}
+        attn = {}
+        v = {}
+        codes = {}
+        z = {}
+        zr = {}
+        stat = {}
+        zn = {}
+        oc = {}
+        ot = {}
+        orow = {}
+
+        def load(g):
+            kb[g] = three.tile([P, SIZES[g] * D], U8, name="kv_bytes")
+            nc.sync.dma_start(out=kb[g][:].rearrange("p (j k) -> p j k", k=D), in_=rows_of(kv_in_bytes, g))
+
+        def load_q(g):
+            q[g] = four.tile([P, SIZES[g], D], BF16, name="q_sb")
+            nc.sync.dma_start(out=q[g][:], in_=rows_of(q_in, g))
+
+        load(0)
+        scale = const.tile([P, 2, D], F32, name="scale")
+        nc.sync.dma_start(out=scale[:, 0, :], in_=kv_in_scale.rearrange("o k -> (o k)").partition_broadcast(P))
+        wv_sb = const.tile([P, T * D], BF16, name="wv_sb")
+        nc.sync.dma_start(out=wv_sb[:].rearrange("m (t k) -> m t k", t=T), in_=w_v.rearrange("(m t) k -> m t k", t=T))
+        awr = const.tile([P, ROWS // P, HEADS], BF16, name="awr")
+        for g0, g1 in ((0, 1), (1, GROUPS - 1), (GROUPS - 1, GROUPS)):
+            n = SIZES[g0]
+            t0, t1 = STARTS[g0], STARTS[g1 - 1] + n
+            nc.sync.dma_start(
+                out=awr[:, t0:t1, :].rearrange("p (g j) h -> p g (j h)", j=n),
+                in_=attn_w[t0 * P : t1 * P].rearrange("(g p j) h o -> p g (j h o)", p=P, j=n),
+            )
+        load(1)
+        bv_raw = const.tile([P, T], BF16, name="bv_raw")
+        nc.sync.dma_start(out=bv_raw[:], in_=b_v.rearrange("(p t) -> p t", t=T))
+        ow_sb = const.tile([P, T * D], BF16, name="ow_sb")
+        nc.sync.dma_start(out=ow_sb[:].rearrange("m (c k) -> m c k", c=T), in_=out_w.rearrange("(c m) k -> m c k", c=T))
+        vecs = const.tile([P, P], BF16, name="vecs")
+        nc.vector.memset(vecs[:], 0.0)
+        for i, vec in enumerate((out_b, ln_g, ln_b)):
+            nc.sync.dma_start(out=vecs[T * i : T * i + T, :], in_=vec.rearrange("(c p) -> c p", c=T))
+        load_q(0)
+
+        ident_f32 = const.tile([P, P], F32, name="ident_f32")
+        make_identity(nc, ident_f32[:])
+        ident_bf = const.tile([P, P], BF16, name="ident_bf")
+        make_identity(nc, ident_bf[:])
+        zero = const.tile([P, 1], F32, name="zero")
+        nc.vector.memset(zero[:], 0.0)
+        eps = const.tile([P, 1], F32, name="eps")
+        nc.vector.tensor_scalar(out=eps[:], in0=zero[:], scalar1=LN_EPS, scalar2=None, op0=ALU.add)
+        warm = const.tile([P, 1], F32, name="warm")
+        nc.scalar.activation(out=warm[:], in_=eps[:], func=ACT.Abs_reciprocal_sqrt, scale=1.0, bias=eps[:])
+
+        def turn(src, h):
+            words = src[:].bitcast(F32)
+            bank = ps_s.tile([P, 2, 2, P], F32, name="bank_s")
+            for j in range(2):
+                first = (2 * h + j) * (D // 2)
+                for u in range(2):
+                    nc.tensor.transpose(bank[:, u, j, :], words[:, first + u : first + D // 2 : 2], ident_f32[:])
+            return bank
+
+        def take_turned(bank, dst, h):
+            nc.scalar.copy(
+                out=dst[:, h * 2 * D : (h + 1) * 2 * D].bitcast(F32).rearrange("p (c u) -> p c u", u=2),
+                in_=bank[:].rearrange("p u j r -> p (j r) u"),
+            )
+
+        def quantise(src, pool, tag):
+            width = src[:].shape[1] // T
+            w = pool.tile([P, width], U32, name=tag + "_codes", align_bytes=64)
+            s = pool.tile([P, width], U8, name=tag + "_scales", align_bytes=64)
+            nc.vector.quantize_mx(out=w[:].bitcast(FP8X4), scales=s[:], in_=src[:])
+            return w, s
+
+        def widen(g, h):
+            if h == 0:
+                kvb[g] = two.tile([P, SIZES[g] * D], BF16, name="kv_bf16")
+            cols = slice(h * 2 * D, (h + 1) * 2 * D)
+            nc.vector.tensor_tensor(
+                out=kvb[g][:, cols],
+                in0=kb[g][:, cols].bitcast(FP8),
+                in1=scale[:].rearrange("p a k -> p (a k)"),
+                op=ALU.mult,
+            )
+
+        def kv_turn(g, h):
+            xt[g, h] = turn(kvb[g], h)
+
+        def kv_take(g, h):
+            if h == 0:
+                grp[g] = two.tile([P, SIZES[g] * D], BF16, name="kv_grouped", align_bytes=64)
+            take_turned(xt[g, h], grp[g], h)
+
+        def kv_quant(g):
+            codes["kv", g] = quantise(grp[g], two, "kv")
+
+        def mm1(g, t):
+            w, s = codes["kv", g]
+            v[g, t] = ps_v.tile([P, SIZES[g] * P], F32, name="bank_v")
+            m = slice(t * P, (t + 1) * P)
+            nc.tensor.matmul_mx(
+                out=v[g, t][:], lhsT=wv_codes[:, m].bitcast(FP8X4), lhsT_scale=wv_scales[:, m],
+                rhs=w[:].bitcast(FP8X4), rhs_scale=s[:], start=True, stop=True,
+            )
+
+        def attn_plane(g, t):
+            if t == 0:
+                attn["plane", g] = two.tile([P, T, SIZES[g] * P], BF16, name="attn_planes")
+            nc.vector.scalar_tensor_tensor(
+                out=attn["plane", g][:, t, :], in0=v[g, t][:], scalar=bv[:, t : t + 1], in1=aw[g][:],
+                op0=ALU.add, op1=ALU.mult,
+            )
+
+        def attn_weave(g, h):
+            if h == 0:
+                attn["grp", g] = two.tile([P, T * SIZES[g] * P], BF16, name="attn_grouped", align_bytes=64)
+            half = 2 * P
+            copy = nc.scalar.copy if g < 2 else nc.vector.tensor_copy
+            copy(
+                out=attn["grp", g][:, h * half * T : (h + 1) * half * T].rearrange("p (r t) -> p r t", t=T),
+                in_=attn["plane", g][:, :, h * half : (h + 1) * half].rearrange("p t r -> p r t"),
+            )
+
+        def attn_quant(g):
+            codes["attn", g] = quantise(attn["grp", g], two, "attn")
+
+        def mm2(g, c):
+            w, s = codes["attn", g]
+            v["y", g, c] = ps_s.tile([P, SIZES[g] * P], F32, name="bank_s")
+            m = slice(c * P, (c + 1) * P)
+            nc.tensor.matmul_mx(
+                out=v["y", g, c][:], lhsT=ow_codes[:, m].bitcast(FP8X4), lhsT_scale=ow_scales[:, m],
+                rhs=w[:].bitcast(FP8X4), rhs_scale=s[:], start=True, stop=True,
+            )
+
+        def y_take(g, c):
+            if c == 0:
+                v["yb", g] = two.tile([P, T, SIZES[g] * P], F32, name="y_cols")
+            nc.scalar.activation(
+                out=v["yb", g][:, c, :], in_=v["y", g, c][:], func=ACT.Identity, bias=cols[:, c : c + 1], scale=1.0
+            )
+
+        def y_turn(g, j):
+            zr[g, j] = ps_v.tile([P, D], F32, name="bank_v")
+            for c in range(T):
+                nc.tensor.transpose(
+                    zr[g, j][:, c * P : (c + 1) * P], v["yb", g][:, c, j * P : (j + 1) * P], ident_f32[:]
+                )
+
+        def residual(g, j):
+            if j == 0:
+                z[g] = three.tile([P, SIZES[g], D], F32, name="z")
+                stat["sum", g] = three.tile([P, SIZES[g]], F32, name="row_sum")
+            nc.vector.scalar_tensor_tensor(
+                out=z[g][:, j, :], in0=zr[g, j][:], scalar=1.0, in1=q[g][:, j, :], op0=ALU.mult, op1=ALU.add,
+                accum_out=stat["sum", g][:, j : j + 1],
+            )
+
+        def squares(g, j):
+            if j == 0:
+                stat["sq", g] = three.tile([P, SIZES[g]], F32, name="row_sq")
+            junk = two.tile([P, D], BF16, name="junk")
+            nc.scalar.activation(
+                out=junk[:], in_=z[g][:, j, :], func=ACT.Square, bias=stat["sum", g][:, j : j + 1], scale=-float(D),
+                accum_out=stat["sq", g][:, j : j + 1],
+            )
+
+        def stats(g):
+            stat["mean", g] = three.tile([P, SIZES[g]], F32, name="row_mean")
+            nc.gpsimd.tensor_scalar(
+                out=stat["mean", g][:], in0=stat["sum", g][:], scalar1=1.0 / D, scalar2=0.0, op0=ALU.mult, op1=ALU.add
+            )
+            stat["rstd", g] = three.tile([P, SIZES[g]], F32, name="row_rstd")
+            nc.scalar.activation(
+                out=stat["rstd", g][:], in_=stat["sq", g][:], func=ACT.Abs_reciprocal_sqrt, bias=eps[:], scale=1.0 / D**3
+            )
+
+        def normalise(g, j):
+            if j == 0:
+                zn[g] = two.tile([P, SIZES[g], D], F32, name="z_norm")
+            nc.vector.tensor_scalar(
+                out=zn[g][:, j, :], in0=z[g][:, j, :], scalar1=stat["mean", g][:, j : j + 1],
+                scalar2=stat["rstd", g][:, j : j + 1], op0=ALU.subtract, op1=ALU.mult,
+            )
+
+        def norm_turn(g, c):
+            oc["ps", g, c] = ps_s.tile([P, SIZES[g] * P], F32, name="bank_s")
+            for j in range(SIZES[g]):
+                nc.tensor.transpose(
+                    oc["ps", g, c][:, j * P : (j + 1) * P], zn[g][:, j, c * P : (c + 1) * P], ident_f32[:]
+                )
+
+        def affine(g, c):
+            if c == 0:
+                oc[g] = two.tile([P, T, SIZES[g] * P], F32, name="out_cols")
+            nc.scalar.activation(
+                out=oc[g][:, c, :], in_=oc["ps", g, c][:], func=ACT.Identity,
+                scale=cols[:, T + c : T + c + 1], bias=cols[:, 2 * T + c : 2 * T + c + 1],
+            )
+
+        def out_turn(g, j):
+            orow[g, j] = ps_s.tile([P, D], F32, name="bank_s")
+            for c in range(T):
+                nc.tensor.transpose(orow[g, j][:, c * P : (c + 1) * P], oc[g][:, c, j * P : (j + 1) * P], ident_f32[:])
+
+        def out_take(g, j):
+            if j == 0:
+                ot[g] = three.tile([P, SIZES[g], D], F32, name="out_sb")
+            copy = nc.vector.tensor_copy if j == 1 and g % 3 == 1 or g >= GROUPS - 3 and j % 2 == 1 else nc.scalar.copy
+            copy(out=ot[g][:, j, :], in_=orow[g, j][:])
+
+        def store(g):
+            nc.sync.dma_start(out=rows_of(out, g), in_=ot[g][:])
+
+        def weights_spread(g):
+            n = SIZES[g] * HEADS
+            aw["x", g] = const.tile([P, n, LANES], BF16, name="aw_spread" + str(g))
+            source = awr[:, STARTS[g] : STARTS[g] + SIZES[g], :].rearrange("p j h -> p (j h)")
+            nc.gpsimd.tensor_scalar(
+                out=aw["x", g][:], in0=source.unsqueeze(2).to_broadcast([P, n, LANES]),
+                scalar1=1.0, scalar2=0.0, op0=ALU.mult, op1=ALU.add,
+            )
+
+        def weights_turn(g):
+            spread = aw["x", g][:].rearrange("p (j h) l -> p j (h l)", h=HEADS)
+            aw["ps", g] = ps_s.tile([P, SIZES[g] * P], BF16, name="bank_s")
+            for j in range(SIZES[g]):
+                nc.tensor.transpose(aw["ps", g][:, j * P : (j + 1) * P], spread[:, j, :], ident_bf[:])
+
+        def weights_take(g):
+            aw[g] = two.tile([P, SIZES[g] * P], BF16, name="aw_sb")
+            nc.scalar.copy(out=aw[g][:], in_=aw["ps", g][:])
+
+        def turn_weights(w_sb):
+            grouped = two.tile([P, T * D], BF16, name="kv_grouped", align_bytes=64)
+            for h in range(2):
+                take_turned(turn(w_sb, h), grouped, h)
+            return grouped
+
+        for g in range(GROUPS):
+            weights_spread(g)
+        nc.vector.tensor_copy(out=scale[:, 1, :], in_=scale[:, 0, :])
+        bv = const.tile([P, T], F32, name="bv")
+        cols = const.tile([P, 3 * T], F32, name="cols")
+
+        for i in range(GROUPS + 4):
+            a, b, c, d, e = i, i - 1, i - 2, i - 3, i - 4
+
+            def live(g):
+                return 0 <= g < GROUPS
+
+            if live(i + 2):
+                load(i + 2)
+            if live(i + 1):
+                load_q(i + 1)
+
+            if live(e):
+                for j in range(SIZES[e]):
+                    out_take(e, j)
+                store(e)
+            if live(b):
+                kv_quant(b)
+                for t in range(T):
+                    mm1(b, t)
+            if i == 2:
+                bank = ps_s.tile([P, P], BF16, name="bank_s")
+                nc.tensor.transpose(bank[:], vecs[:], ident_bf[:])
+                nc.vector.tensor_copy(out=cols[:], in_=bank[:, : 3 * T])
+            if live(c):
+                attn_quant(c)
+                for k in range(T):
+                    mm2(c, k)
+                    y_take(c, k)
+            if live(d):
+                for j in range(SIZES[d]):
+                    normalise(d, j)
+                for k in range(T):
+                    norm_turn(d, k)
+                    affine(d, k)
+            if live(a):
+                for h in range(SIZES[a] // 2):
+                    widen(a, h)
+            if i == 0:
+                wv_codes, wv_scales = quantise(turn_weights(wv_sb), const, "wv")
+                nc.vector.tensor_copy(out=bv[:], in_=bv_raw[:])
+            if live(b):
+                for t in range(T):
+                    attn_plane(b, t)
+            if i == 1:
+                ow_codes, ow_scales = quantise(turn_weights(ow_sb), const, "ow")
+            for j in range(T):
+                if live(c) and j < SIZES[c]:
+                    y_turn(c, j)
+                if live(a):
+                    if j < SIZES[a] // 2:
+                        kv_turn(a, j)
+                        kv_take(a, j)
+                    elif j == 2:
+                        weights_turn(a)
+                        weights_take(a)
+            if live(c):
+                for j in range(SIZES[c]):
+                    residual(c, j)
+                    squares(c, j)
+                stats(c)
+            if live(d):
+                for j in range(SIZES[d]):
+                    out_turn(d, j)
+            if live(b):
+                for h in range(SIZES[b] // 2):
+                    attn_weave(b, h)

@@ -19,7 +19,7 @@ ALU = mybir.AluOpType
 P = 128
 T = 4
 LANES = P // HEADS
-SIZES = (2,) + (4,) * 15 + (2,)
+SIZES = (2, 4, 4, 4, 4, 4, 4, 4, 4, 4, 4, 4, 4, 4, 4, 4, 2)
 GROUPS = len(SIZES)
 STARTS = tuple(sum(SIZES[:g]) for g in range(GROUPS))
 
@@ -72,7 +72,7 @@ def tile_crossmodalattention_pa_t_kernel(
         wv_sb = const.tile([P, T * D], BF16, name="wv_sb")
         nc.sync.dma_start(out=wv_sb[:].rearrange("m (t k) -> m t k", t=T), in_=w_v.rearrange("(m t) k -> m t k", t=T))
         awr = const.tile([P, ROWS // P, HEADS], BF16, name="awr")
-        for g0, g1 in ((0, 1), (1, GROUPS - 1), (GROUPS - 1, GROUPS)):
+        for g0, g1 in ((0, 1), (1, 16), (16, 17)):
             n = SIZES[g0]
             t0, t1 = STARTS[g0], STARTS[g1 - 1] + n
             nc.sync.dma_start(
@@ -124,7 +124,7 @@ def tile_crossmodalattention_pa_t_kernel(
             return w, s
 
         def widen(g, h):
-            if h == 0:
+            if g not in kvb:
                 kvb[g] = two.tile([P, SIZES[g] * D], BF16, name="kv_bf16")
             cols = slice(h * 2 * D, (h + 1) * 2 * D)
             nc.vector.tensor_tensor(
@@ -138,7 +138,7 @@ def tile_crossmodalattention_pa_t_kernel(
             xt[g, h] = turn(kvb[g], h)
 
         def kv_take(g, h):
-            if h == 0:
+            if g not in grp:
                 grp[g] = two.tile([P, SIZES[g] * D], BF16, name="kv_grouped", align_bytes=64)
             take_turned(xt[g, h], grp[g], h)
 
@@ -155,7 +155,7 @@ def tile_crossmodalattention_pa_t_kernel(
             )
 
         def attn_plane(g, t):
-            if t == 0:
+            if ("plane", g) not in attn:
                 attn["plane", g] = two.tile([P, T, SIZES[g] * P], BF16, name="attn_planes")
             nc.vector.scalar_tensor_tensor(
                 out=attn["plane", g][:, t, :], in0=v[g, t][:], scalar=bv[:, t : t + 1], in1=aw[g][:],
@@ -163,7 +163,7 @@ def tile_crossmodalattention_pa_t_kernel(
             )
 
         def attn_weave(g, h):
-            if h == 0:
+            if ("grp", g) not in attn:
                 attn["grp", g] = two.tile([P, T * SIZES[g] * P], BF16, name="attn_grouped", align_bytes=64)
             half = 2 * P
             copy = nc.scalar.copy if g < 2 else nc.vector.tensor_copy
@@ -185,7 +185,7 @@ def tile_crossmodalattention_pa_t_kernel(
             )
 
         def y_take(g, c):
-            if c == 0:
+            if ("yb", g) not in v:
                 v["yb", g] = two.tile([P, T, SIZES[g] * P], F32, name="y_cols")
             nc.scalar.activation(
                 out=v["yb", g][:, c, :], in_=v["y", g, c][:], func=ACT.Identity, bias=cols[:, c : c + 1], scale=1.0
@@ -199,7 +199,7 @@ def tile_crossmodalattention_pa_t_kernel(
                 )
 
         def residual(g, j):
-            if j == 0:
+            if g not in z:
                 z[g] = three.tile([P, SIZES[g], D], F32, name="z")
                 stat["sum", g] = three.tile([P, SIZES[g]], F32, name="row_sum")
             nc.vector.scalar_tensor_tensor(
@@ -208,7 +208,7 @@ def tile_crossmodalattention_pa_t_kernel(
             )
 
         def squares(g, j):
-            if j == 0:
+            if ("sq", g) not in stat:
                 stat["sq", g] = three.tile([P, SIZES[g]], F32, name="row_sq")
             junk = two.tile([P, D], BF16, name="junk")
             nc.scalar.activation(
@@ -227,7 +227,7 @@ def tile_crossmodalattention_pa_t_kernel(
             )
 
         def normalise(g, j):
-            if j == 0:
+            if g not in zn:
                 zn[g] = two.tile([P, SIZES[g], D], F32, name="z_norm")
             nc.vector.tensor_scalar(
                 out=zn[g][:, j, :], in0=z[g][:, j, :], scalar1=stat["mean", g][:, j : j + 1],
@@ -242,7 +242,7 @@ def tile_crossmodalattention_pa_t_kernel(
                 )
 
         def affine(g, c):
-            if c == 0:
+            if g not in oc:
                 oc[g] = two.tile([P, T, SIZES[g] * P], F32, name="out_cols")
             nc.scalar.activation(
                 out=oc[g][:, c, :], in_=oc["ps", g, c][:], func=ACT.Identity,
@@ -255,9 +255,9 @@ def tile_crossmodalattention_pa_t_kernel(
                 nc.tensor.transpose(orow[g, j][:, c * P : (c + 1) * P], oc[g][:, c, j * P : (j + 1) * P], ident_f32[:])
 
         def out_take(g, j):
-            if j == 0:
+            if g not in ot:
                 ot[g] = three.tile([P, SIZES[g], D], F32, name="out_sb")
-            copy = nc.vector.tensor_copy if j == 1 and g % 3 == 1 or g >= GROUPS - 3 and j % 2 == 1 else nc.scalar.copy
+            copy = nc.vector.tensor_copy if g >= GROUPS - 4 and j % 2 or g % 4 == 1 and j == 1 else nc.scalar.copy
             copy(out=ot[g][:, j, :], in_=orow[g, j][:])
 
         def store(g):
@@ -294,69 +294,137 @@ def tile_crossmodalattention_pa_t_kernel(
         bv = const.tile([P, T], F32, name="bv")
         cols = const.tile([P, 3 * T], F32, name="cols")
 
+        def live(g):
+            return 0 <= g < GROUPS
+
+        def columns():
+            bank = ps_s.tile([P, P], BF16, name="bank_s")
+            nc.tensor.transpose(bank[:], vecs[:], ident_bf[:])
+            nc.vector.tensor_copy(out=cols[:], in_=bank[:, : 3 * T])
+
         for i in range(GROUPS + 4):
-            a, b, c, d, e = i, i - 1, i - 2, i - 3, i - 4
-
-            def live(g):
-                return 0 <= g < GROUPS
-
             if live(i + 2):
                 load(i + 2)
             if live(i + 1):
                 load_q(i + 1)
-
-            if live(e):
-                for j in range(SIZES[e]):
-                    out_take(e, j)
-                store(e)
-            if live(b):
-                kv_quant(b)
-                for t in range(T):
-                    mm1(b, t)
-            if i == 2:
-                bank = ps_s.tile([P, P], BF16, name="bank_s")
-                nc.tensor.transpose(bank[:], vecs[:], ident_bf[:])
-                nc.vector.tensor_copy(out=cols[:], in_=bank[:, : 3 * T])
-            if live(c):
-                attn_quant(c)
-                for k in range(T):
-                    mm2(c, k)
-                    y_take(c, k)
-            if live(d):
-                for j in range(SIZES[d]):
-                    normalise(d, j)
-                for k in range(T):
-                    norm_turn(d, k)
-                    affine(d, k)
-            if live(a):
-                for h in range(SIZES[a] // 2):
-                    widen(a, h)
+            if live(i - 3):
+                residual(i - 3, 0)
+            if live(i - 1):
+                weights_take(i - 1)
+            if live(i - 0):
+                widen(i - 0, 0)
             if i == 0:
-                wv_codes, wv_scales = quantise(turn_weights(wv_sb), const, "wv")
-                nc.vector.tensor_copy(out=bv[:], in_=bv_raw[:])
-            if live(b):
-                for t in range(T):
-                    attn_plane(b, t)
+                wv_grouped = turn_weights(wv_sb)
+            if live(i - 2):
+                attn_quant(i - 2)
+            if live(i - 4):
+                out_turn(i - 4, 0)
+                out_turn(i - 4, 1)
+                out_take(i - 4, 0)
+            if live(i - 4) and SIZES[i - 4] == 4:
+                out_turn(i - 4, 3)
+            if live(i - 3) and SIZES[i - 3] == 4:
+                squares(i - 3, 2)
+            if live(i - 4) and SIZES[i - 4] == 4:
+                out_turn(i - 4, 2)
+            if live(i - 3):
+                squares(i - 3, 0)
+            if live(i - 4):
+                out_take(i - 4, 1)
+            if live(i - 3):
+                stats(i - 3)
+            if live(i - 0) and SIZES[i - 0] == 4:
+                widen(i - 0, 1)
+            if live(i - 1):
+                mm1(i - 1, 2)
+            if live(i - 4) and SIZES[i - 4] == 4:
+                out_take(i - 4, 3)
+            if live(i - 1):
+                mm1(i - 1, 0)
+            if i == 2:
+                columns()
+            if live(i - 2):
+                mm2(i - 2, 0)
+            if live(i - 4) and SIZES[i - 4] == 4:
+                out_take(i - 4, 2)
+            if live(i - 3):
+                normalise(i - 3, 0)
+            if live(i - 3) and SIZES[i - 3] == 4:
+                normalise(i - 3, 3)
+                normalise(i - 3, 2)
+            if live(i - 3):
+                normalise(i - 3, 1)
+            if live(i - 2):
+                y_take(i - 2, 0)
+                mm2(i - 2, 2)
             if i == 1:
-                ow_codes, ow_scales = quantise(turn_weights(ow_sb), const, "ow")
-            for j in range(T):
-                if live(c) and j < SIZES[c]:
-                    y_turn(c, j)
-                if live(a):
-                    if j < SIZES[a] // 2:
-                        kv_turn(a, j)
-                        kv_take(a, j)
-                    elif j == 2:
-                        weights_turn(a)
-                        weights_take(a)
-            if live(c):
-                for j in range(SIZES[c]):
-                    residual(c, j)
-                    squares(c, j)
-                stats(c)
-            if live(d):
-                for j in range(SIZES[d]):
-                    out_turn(d, j)
-            if live(b):
-                for h in range(SIZES[b] // 2):
-                    attn_weave(b, h)
+                nc.vector.tensor_copy(out=bv[:], in_=bv_raw[:])
+            if live(i - 1):
+                attn_plane(i - 1, 2)
+            if live(i - 2):
+                y_take(i - 2, 2)
+                mm2(i - 2, 3)
+                y_take(i - 2, 3)
+            if live(i - 1):
+                mm1(i - 1, 3)
+            if live(i - 2):
+                mm2(i - 2, 1)
+            if live(i - 1):
+                attn_plane(i - 1, 3)
+            if live(i - 2):
+                y_take(i - 2, 1)
+            if live(i - 1):
+                mm1(i - 1, 1)
+                attn_plane(i - 1, 1)
+            if live(i - 3):
+                norm_turn(i - 3, 2)
+                affine(i - 3, 2)
+                norm_turn(i - 3, 1)
+                affine(i - 3, 1)
+            if live(i - 1):
+                attn_plane(i - 1, 0)
+            if live(i - 2):
+                y_turn(i - 2, 1)
+            if live(i - 0):
+                kv_turn(i - 0, 0)
+                kv_take(i - 0, 0)
+            if live(i - 3):
+                norm_turn(i - 3, 0)
+                affine(i - 3, 0)
+            if i == 0:
+                wv_codes, wv_scales = quantise(wv_grouped, const, "wv")
+            if live(i - 2) and SIZES[i - 2] == 4:
+                y_turn(i - 2, 3)
+            if live(i - 2):
+                residual(i - 2, 1)
+            if live(i - 0) and SIZES[i - 0] == 4:
+                kv_turn(i - 0, 1)
+                kv_take(i - 0, 1)
+            if live(i - 1) and SIZES[i - 1] == 4:
+                attn_weave(i - 1, 1)
+            if live(i - 3):
+                norm_turn(i - 3, 3)
+                affine(i - 3, 3)
+            if i == 1:
+                ow_codes, ow_scales = quantise(ow_grouped, const, "ow")
+            if live(i - 4):
+                store(i - 4)
+            if live(i - 2) and SIZES[i - 2] == 4:
+                residual(i - 2, 3)
+            if live(i - 1):
+                attn_weave(i - 1, 0)
+            if live(i - 2):
+                squares(i - 2, 1)
+            if live(i - 0):
+                kv_quant(i - 0)
+            if live(i - 2):
+                y_turn(i - 2, 0)
+            if live(i - 2) and SIZES[i - 2] == 4:
+                y_turn(i - 2, 2)
+                residual(i - 2, 2)
+            if i == 0:
+                ow_grouped = turn_weights(ow_sb)
+            if live(i - 2) and SIZES[i - 2] == 4:
+                squares(i - 2, 3)
+            if live(i - 0):
+                weights_turn(i - 0)

from contextlib import ExitStack

import concourse.mybir as mybir
from concourse.masks import make_identity

ROWS, D, HEADS = 8192, 512, 8
FLOPS = 2 * 2 * ROWS * D * D
LN_EPS = 1e-5

F32 = mybir.dt.float32
BF16 = mybir.dt.bfloat16
U32 = mybir.dt.uint32
U8 = mybir.dt.uint8
FP8 = mybir.dt.float8_e4m3fn
FP8X4 = mybir.dt.float8_e4m3fn_x4
ACT = mybir.ActivationFunctionType
ALU = mybir.AluOpType

P = 128
T = 4
LANES = P // HEADS
SIZES = (2, 4, 4, 4, 4, 4, 4, 4, 4, 4, 4, 4, 4, 4, 4, 4, 2)
GROUPS = len(SIZES)
STARTS = tuple(sum(SIZES[:g]) for g in range(GROUPS))


def tile_crossmodalattention_pa_t_kernel(
    tc, kv_in_bytes, kv_in_scale, q_in, attn_w, w_v, b_v, out_w, out_b, ln_g, ln_b, out
):
    nc = tc.nc

    def rows_of(tensor, g):
        return tensor[STARTS[g] * P : (STARTS[g] + SIZES[g]) * P, :].rearrange("(p j) n -> p j n", j=SIZES[g])

    with ExitStack() as ctx:
        const = ctx.enter_context(tc.tile_pool(name="const", bufs=1))
        two = ctx.enter_context(tc.tile_pool(name="two", bufs=2))
        three = ctx.enter_context(tc.tile_pool(name="three", bufs=3))
        four = ctx.enter_context(tc.tile_pool(name="four", bufs=4))
        ps_s = ctx.enter_context(tc.psum_pool(name="ps_s", bufs=4))
        ps_v = ctx.enter_context(tc.psum_pool(name="ps_v", bufs=4))
        ctx.enter_context(tc.manual_schedule())

        kb = {}
        q = {}
        kvb = {}
        xt = {}
        grp = {}
        aw = {}
        attn = {}
        v = {}
        codes = {}
        z = {}
        zr = {}
        stat = {}
        zn = {}
        oc = {}
        ot = {}
        orow = {}

        def load(g):
            kb[g] = three.tile([P, SIZES[g] * D], U8, name="kv_bytes")
            nc.sync.dma_start(out=kb[g][:].rearrange("p (j k) -> p j k", k=D), in_=rows_of(kv_in_bytes, g))

        def load_q(g):
            q[g] = four.tile([P, SIZES[g], D], BF16, name="q_sb")
            nc.sync.dma_start(out=q[g][:], in_=rows_of(q_in, g))

        load(0)
        scale = const.tile([P, 2, D], F32, name="scale")
        nc.sync.dma_start(out=scale[:, 0, :], in_=kv_in_scale.rearrange("o k -> (o k)").partition_broadcast(P))
        wv_sb = const.tile([P, T * D], BF16, name="wv_sb")
        nc.sync.dma_start(out=wv_sb[:].rearrange("m (t k) -> m t k", t=T), in_=w_v.rearrange("(m t) k -> m t k", t=T))
        awr = const.tile([P, ROWS // P, HEADS], BF16, name="awr")
        for g0, g1 in ((0, 1), (1, 16), (16, 17)):
            n = SIZES[g0]
            t0, t1 = STARTS[g0], STARTS[g1 - 1] + n
            nc.sync.dma_start(
                out=awr[:, t0:t1, :].rearrange("p (g j) h -> p g (j h)", j=n),
                in_=attn_w[t0 * P : t1 * P].rearrange("(g p j) h o -> p g (j h o)", p=P, j=n),
            )
        load(1)
        bv_raw = const.tile([P, T], BF16, name="bv_raw")
        nc.sync.dma_start(out=bv_raw[:], in_=b_v.rearrange("(p t) -> p t", t=T))
        ow_sb = const.tile([P, T * D], BF16, name="ow_sb")
        nc.sync.dma_start(out=ow_sb[:].rearrange("m (c k) -> m c k", c=T), in_=out_w.rearrange("(c m) k -> m c k", c=T))
        vecs = const.tile([P, P], BF16, name="vecs")
        nc.vector.memset(vecs[:], 0.0)
        for i, vec in enumerate((out_b, ln_g, ln_b)):
            nc.sync.dma_start(out=vecs[T * i : T * i + T, :], in_=vec.rearrange("(c p) -> c p", c=T))
        load_q(0)

        ident_f32 = const.tile([P, P], F32, name="ident_f32")
        make_identity(nc, ident_f32[:])
        ident_bf = const.tile([P, P], BF16, name="ident_bf")
        make_identity(nc, ident_bf[:])
        zero = const.tile([P, 1], F32, name="zero")
        nc.vector.memset(zero[:], 0.0)
        eps = const.tile([P, 1], F32, name="eps")
        nc.vector.tensor_scalar(out=eps[:], in0=zero[:], scalar1=LN_EPS, scalar2=None, op0=ALU.add)
        warm = const.tile([P, 1], F32, name="warm")
        nc.scalar.activation(out=warm[:], in_=eps[:], func=ACT.Abs_reciprocal_sqrt, scale=1.0, bias=eps[:])

        def turn(src, h):
            words = src[:].bitcast(F32)
            bank = ps_s.tile([P, 2, 2, P], F32, name="bank_s")
            for j in range(2):
                first = (2 * h + j) * (D // 2)
                for u in range(2):
                    nc.tensor.transpose(bank[:, u, j, :], words[:, first + u : first + D // 2 : 2], ident_f32[:])
            return bank

        def take_turned(bank, dst, h):
            nc.scalar.copy(
                out=dst[:, h * 2 * D : (h + 1) * 2 * D].bitcast(F32).rearrange("p (c u) -> p c u", u=2),
                in_=bank[:].rearrange("p u j r -> p (j r) u"),
            )

        def quantise(src, pool, tag):
            width = src[:].shape[1] // T
            w = pool.tile([P, width], U32, name=tag + "_codes", align_bytes=64)
            s = pool.tile([P, width], U8, name=tag + "_scales", align_bytes=64)
            nc.vector.quantize_mx(out=w[:].bitcast(FP8X4), scales=s[:], in_=src[:])
            return w, s

        def widen(g, h):
            if g not in kvb:
                kvb[g] = two.tile([P, SIZES[g] * D], BF16, name="kv_bf16")
            cols = slice(h * 2 * D, (h + 1) * 2 * D)
            nc.vector.tensor_tensor(
                out=kvb[g][:, cols],
                in0=kb[g][:, cols].bitcast(FP8),
                in1=scale[:].rearrange("p a k -> p (a k)"),
                op=ALU.mult,
            )

        def kv_turn(g, h):
            xt[g, h] = turn(kvb[g], h)

        def kv_take(g, h):
            if g not in grp:
                grp[g] = two.tile([P, SIZES[g] * D], BF16, name="kv_grouped", align_bytes=64)
            take_turned(xt[g, h], grp[g], h)

        def kv_quant(g):
            codes["kv", g] = quantise(grp[g], two, "kv")

        def mm1(g, t):
            w, s = codes["kv", g]
            v[g, t] = ps_v.tile([P, SIZES[g] * P], F32, name="bank_v")
            m = slice(t * P, (t + 1) * P)
            nc.tensor.matmul_mx(
                out=v[g, t][:], lhsT=wv_codes[:, m].bitcast(FP8X4), lhsT_scale=wv_scales[:, m],
                rhs=w[:].bitcast(FP8X4), rhs_scale=s[:], start=True, stop=True,
            )

        def attn_plane(g, t):
            if ("plane", g) not in attn:
                attn["plane", g] = two.tile([P, T, SIZES[g] * P], BF16, name="attn_planes")
            nc.vector.scalar_tensor_tensor(
                out=attn["plane", g][:, t, :], in0=v[g, t][:], scalar=bv[:, t : t + 1], in1=aw[g][:],
                op0=ALU.add, op1=ALU.mult,
            )

        def attn_weave(g, h):
            if ("grp", g) not in attn:
                attn["grp", g] = two.tile([P, T * SIZES[g] * P], BF16, name="attn_grouped", align_bytes=64)
            half = 2 * P
            copy = nc.scalar.copy if g < 2 else nc.vector.tensor_copy
            copy(
                out=attn["grp", g][:, h * half * T : (h + 1) * half * T].rearrange("p (r t) -> p r t", t=T),
                in_=attn["plane", g][:, :, h * half : (h + 1) * half].rearrange("p t r -> p r t"),
            )

        def attn_quant(g):
            codes["attn", g] = quantise(attn["grp", g], two, "attn")

        def mm2(g, c):
            w, s = codes["attn", g]
            v["y", g, c] = ps_s.tile([P, SIZES[g] * P], F32, name="bank_s")
            m = slice(c * P, (c + 1) * P)
            nc.tensor.matmul_mx(
                out=v["y", g, c][:], lhsT=ow_codes[:, m].bitcast(FP8X4), lhsT_scale=ow_scales[:, m],
                rhs=w[:].bitcast(FP8X4), rhs_scale=s[:], start=True, stop=True,
            )

        def y_take(g, c):
            if ("yb", g) not in v:
                v["yb", g] = two.tile([P, T, SIZES[g] * P], F32, name="y_cols")
            nc.scalar.activation(
                out=v["yb", g][:, c, :], in_=v["y", g, c][:], func=ACT.Identity, bias=cols[:, c : c + 1], scale=1.0
            )

        def y_turn(g, j):
            zr[g, j] = ps_v.tile([P, D], F32, name="bank_v")
            for c in range(T):
                nc.tensor.transpose(
                    zr[g, j][:, c * P : (c + 1) * P], v["yb", g][:, c, j * P : (j + 1) * P], ident_f32[:]
                )

        def residual(g, j):
            if g not in z:
                z[g] = three.tile([P, SIZES[g], D], F32, name="z")
                stat["sum", g] = three.tile([P, SIZES[g]], F32, name="row_sum")
            nc.vector.scalar_tensor_tensor(
                out=z[g][:, j, :], in0=zr[g, j][:], scalar=1.0, in1=q[g][:, j, :], op0=ALU.mult, op1=ALU.add,
                accum_out=stat["sum", g][:, j : j + 1],
            )

        def squares(g, j):
            if ("sq", g) not in stat:
                stat["sq", g] = three.tile([P, SIZES[g]], F32, name="row_sq")
            junk = two.tile([P, D], BF16, name="junk")
            nc.scalar.activation(
                out=junk[:], in_=z[g][:, j, :], func=ACT.Square, bias=stat["sum", g][:, j : j + 1], scale=-float(D),
                accum_out=stat["sq", g][:, j : j + 1],
            )

        def stats(g):
            stat["mean", g] = three.tile([P, SIZES[g]], F32, name="row_mean")
            nc.gpsimd.tensor_scalar(
                out=stat["mean", g][:], in0=stat["sum", g][:], scalar1=1.0 / D, scalar2=0.0, op0=ALU.mult, op1=ALU.add
            )
            stat["rstd", g] = three.tile([P, SIZES[g]], F32, name="row_rstd")
            nc.scalar.activation(
                out=stat["rstd", g][:], in_=stat["sq", g][:], func=ACT.Abs_reciprocal_sqrt, bias=eps[:], scale=1.0 / D**3
            )

        def normalise(g, j):
            if g not in zn:
                zn[g] = two.tile([P, SIZES[g], D], F32, name="z_norm")
            nc.vector.tensor_scalar(
                out=zn[g][:, j, :], in0=z[g][:, j, :], scalar1=stat["mean", g][:, j : j + 1],
                scalar2=stat["rstd", g][:, j : j + 1], op0=ALU.subtract, op1=ALU.mult,
            )

        def norm_turn(g, c):
            oc["ps", g, c] = ps_s.tile([P, SIZES[g] * P], F32, name="bank_s")
            for j in range(SIZES[g]):
                nc.tensor.transpose(
                    oc["ps", g, c][:, j * P : (j + 1) * P], zn[g][:, j, c * P : (c + 1) * P], ident_f32[:]
                )

        def affine(g, c):
            if g not in oc:
                oc[g] = two.tile([P, T, SIZES[g] * P], F32, name="out_cols")
            nc.scalar.activation(
                out=oc[g][:, c, :], in_=oc["ps", g, c][:], func=ACT.Identity,
                scale=cols[:, T + c : T + c + 1], bias=cols[:, 2 * T + c : 2 * T + c + 1],
            )

        def out_turn(g, j):
            orow[g, j] = ps_s.tile([P, D], F32, name="bank_s")
            for c in range(T):
                nc.tensor.transpose(orow[g, j][:, c * P : (c + 1) * P], oc[g][:, c, j * P : (j + 1) * P], ident_f32[:])

        def out_take(g, j):
            if g not in ot:
                ot[g] = three.tile([P, SIZES[g], D], F32, name="out_sb")
            copy = nc.vector.tensor_copy if g >= GROUPS - 4 and j % 2 or g % 4 == 1 and j == 1 else nc.scalar.copy
            copy(out=ot[g][:, j, :], in_=orow[g, j][:])

        def store(g):
            nc.sync.dma_start(out=rows_of(out, g), in_=ot[g][:])

        def weights_spread(g):
            n = SIZES[g] * HEADS
            aw["x", g] = const.tile([P, n, LANES], BF16, name="aw_spread" + str(g))
            source = awr[:, STARTS[g] : STARTS[g] + SIZES[g], :].rearrange("p j h -> p (j h)")
            nc.gpsimd.tensor_scalar(
                out=aw["x", g][:], in0=source.unsqueeze(2).to_broadcast([P, n, LANES]),
                scalar1=1.0, scalar2=0.0, op0=ALU.mult, op1=ALU.add,
            )

        def weights_turn(g):
            spread = aw["x", g][:].rearrange("p (j h) l -> p j (h l)", h=HEADS)
            aw["ps", g] = ps_s.tile([P, SIZES[g] * P], BF16, name="bank_s")
            for j in range(SIZES[g]):
                nc.tensor.transpose(aw["ps", g][:, j * P : (j + 1) * P], spread[:, j, :], ident_bf[:])

        def weights_take(g):
            aw[g] = two.tile([P, SIZES[g] * P], BF16, name="aw_sb")
            nc.scalar.copy(out=aw[g][:], in_=aw["ps", g][:])

        def turn_weights(w_sb):
            grouped = two.tile([P, T * D], BF16, name="kv_grouped", align_bytes=64)
            for h in range(2):
                take_turned(turn(w_sb, h), grouped, h)
            return grouped

        for g in range(GROUPS):
            weights_spread(g)
        nc.vector.tensor_copy(out=scale[:, 1, :], in_=scale[:, 0, :])
        bv = const.tile([P, T], F32, name="bv")
        cols = const.tile([P, 3 * T], F32, name="cols")

        def live(g):
            return 0 <= g < GROUPS

        def columns():
            bank = ps_s.tile([P, P], BF16, name="bank_s")
            nc.tensor.transpose(bank[:], vecs[:], ident_bf[:])
            nc.vector.tensor_copy(out=cols[:], in_=bank[:, : 3 * T])

        for i in range(GROUPS + 4):
            if live(i + 2):
                load(i + 2)
            if live(i + 1):
                load_q(i + 1)
            if live(i - 3):
                residual(i - 3, 0)
            if live(i - 1):
                weights_take(i - 1)
            if live(i - 0):
                widen(i - 0, 0)
            if i == 0:
                wv_grouped = turn_weights(wv_sb)
            if live(i - 2):
                attn_quant(i - 2)
            if live(i - 4):
                out_turn(i - 4, 0)
                out_turn(i - 4, 1)
                out_take(i - 4, 0)
            if live(i - 4) and SIZES[i - 4] == 4:
                out_turn(i - 4, 3)
            if live(i - 3) and SIZES[i - 3] == 4:
                squares(i - 3, 2)
            if live(i - 4) and SIZES[i - 4] == 4:
                out_turn(i - 4, 2)
            if live(i - 3):
                squares(i - 3, 0)
            if live(i - 4):
                out_take(i - 4, 1)
            if live(i - 3):
                stats(i - 3)
            if live(i - 0) and SIZES[i - 0] == 4:
                widen(i - 0, 1)
            if live(i - 1):
                mm1(i - 1, 2)
            if live(i - 4) and SIZES[i - 4] == 4:
                out_take(i - 4, 3)
            if live(i - 1):
                mm1(i - 1, 0)
            if i == 2:
                columns()
            if live(i - 2):
                mm2(i - 2, 0)
            if live(i - 4) and SIZES[i - 4] == 4:
                out_take(i - 4, 2)
            if live(i - 3):
                normalise(i - 3, 0)
            if live(i - 3) and SIZES[i - 3] == 4:
                normalise(i - 3, 3)
                normalise(i - 3, 2)
            if live(i - 3):
                normalise(i - 3, 1)
            if live(i - 2):
                y_take(i - 2, 0)
                mm2(i - 2, 2)
            if i == 1:
                nc.vector.tensor_copy(out=bv[:], in_=bv_raw[:])
            if live(i - 1):
                attn_plane(i - 1, 2)
            if live(i - 2):
                y_take(i - 2, 2)
                mm2(i - 2, 3)
                y_take(i - 2, 3)
            if live(i - 1):
                mm1(i - 1, 3)
            if live(i - 2):
                mm2(i - 2, 1)
            if live(i - 1):
                attn_plane(i - 1, 3)
            if live(i - 2):
                y_take(i - 2, 1)
            if live(i - 1):
                mm1(i - 1, 1)
                attn_plane(i - 1, 1)
            if live(i - 3):
                norm_turn(i - 3, 2)
                affine(i - 3, 2)
                norm_turn(i - 3, 1)
                affine(i - 3, 1)
            if live(i - 1):
                attn_plane(i - 1, 0)
            if live(i - 2):
                y_turn(i - 2, 1)
            if live(i - 0):
                kv_turn(i - 0, 0)
                kv_take(i - 0, 0)
            if live(i - 3):
                norm_turn(i - 3, 0)
                affine(i - 3, 0)
            if i == 0:
                wv_codes, wv_scales = quantise(wv_grouped, const, "wv")
            if live(i - 2) and SIZES[i - 2] == 4:
                y_turn(i - 2, 3)
            if live(i - 2):
                residual(i - 2, 1)
            if live(i - 0) and SIZES[i - 0] == 4:
                kv_turn(i - 0, 1)
                kv_take(i - 0, 1)
            if live(i - 1) and SIZES[i - 1] == 4:
                attn_weave(i - 1, 1)
            if live(i - 3):
                norm_turn(i - 3, 3)
                affine(i - 3, 3)
            if i == 1:
                ow_codes, ow_scales = quantise(ow_grouped, const, "ow")
            if live(i - 4):
                store(i - 4)
            if live(i - 2) and SIZES[i - 2] == 4:
                residual(i - 2, 3)
            if live(i - 1):
                attn_weave(i - 1, 0)
            if live(i - 2):
                squares(i - 2, 1)
            if live(i - 0):
                kv_quant(i - 0)
            if live(i - 2):
                y_turn(i - 2, 0)
            if live(i - 2) and SIZES[i - 2] == 4:
                y_turn(i - 2, 2)
                residual(i - 2, 2)
            if i == 0:
                ow_grouped = turn_weights(ow_sb)
            if live(i - 2) and SIZES[i - 2] == 4:
                squares(i - 2, 3)
            if live(i - 0):
                weights_turn(i - 0)
